import numpy as np
import ml_dtypes


def mxq(x, axis, fmt="e4m3"):
    dtype, down = {"e4m3": (ml_dtypes.float8_e4m3fn, 7), "e5m2": (ml_dtypes.float8_e5m2, 14)}[fmt]
    v = np.moveaxis(np.asarray(x, np.float32).astype(ml_dtypes.bfloat16).astype(np.float64), axis, -1)
    blocks = v.reshape(v.shape[:-1] + (-1, 32))
    amax = np.abs(blocks).max(-1, keepdims=True)
    byte = np.maximum(np.where(amax > 0, np.frexp(amax)[1] - 1 + 127, 0) - down, 1)
    scale = np.exp2(byte - 127.0)
    codes = (blocks / scale).astype(np.float32).astype(dtype).astype(np.float64)
    return np.moveaxis((codes * scale).reshape(v.shape), -1, axis)


WIDE = False


def mx_kscale(k):
    if not WIDE:
        return np.ones(k)
    levels = np.array([10, -10, 5, -5, 0])
    if k % 512:
        return np.exp2(np.random.permutation(np.resize(levels, k // 32))).repeat(32)
    a = np.empty((k // 512, 16))
    for p in range(k // 512):
        a[p, :8] = np.random.permutation(np.resize(levels, 8))
        for g in range(8):
            far = levels[np.abs(levels - a[p, g]) >= 10]
            a[p, g + 8] = far[np.random.randint(len(far))]
    return np.exp2(a.ravel()).repeat(32)


BF16 = ml_dtypes.bfloat16


def bf(x):
    return np.asarray(x, np.float32).astype(BF16)


def f64(x):
    return np.asarray(x).astype(np.float64)


N, H, S, R, T = 4096, 512, 4, 128, 128


def sigmoid(v):
    return 1.0 / (1.0 + np.exp(-v))


def setup_inputs():
    s, t = mx_kscale(H), mx_kscale(H)
    g = np.exp(np.random.standard_normal((S, N)))
    return {"encodings": bf(np.random.standard_normal((N, H)) * s),
            "alphas": bf(g / g.sum(axis=0, keepdims=True)),
            "W1": bf(np.random.standard_normal((S, H, H)) * 1.4 / np.sqrt(H) / s[None, :, None] * t[None, None, :]),
            "b1": bf(np.random.standard_normal((S, H)) * 0.3 * t[None, :]),
            "W2": bf(np.random.standard_normal((S, H, T)) * 2.0 / np.sqrt(H) / t[None, :, None]),
            "b2": bf(np.random.standard_normal((S, T)) * 0.5)}


def reference(encodings, alphas, W1, b1, W2, b2):
    h0 = np.maximum(f64(encodings), 0.0)
    h1 = np.maximum((mxq(h0, 1, "e4m3") @ mxq(f64(W1), 1, "e4m3")) + f64(b1)[:, None, :], 0.0)
    out = sigmoid((mxq(h1, 2, "e4m3") @ mxq(f64(W2), 1, "e4m3")) + f64(b2)[:, None, :])
    return np.sum(f64(alphas)[:, :, None] * out, axis=0)

@@ -1,0 +1,423 @@
+from contextlib import ExitStack
+
+import concourse.masks as masks
+import concourse.mybir as mybir
+
+N_TOK, H, S, T = 4096, 512, 4, 128
+FLOPS = 2 * N_TOK * H * H * S + 2 * N_TOK * H * T * S
+
+F32 = mybir.dt.float32
+BF16 = mybir.dt.bfloat16
+U32 = mybir.dt.uint32
+U8 = mybir.dt.uint8
+FP8X4 = mybir.dt.float8_e4m3fn_x4
+ACT = mybir.ActivationFunctionType
+ALU = mybir.AluOpType
+
+P = 128
+PACK = 4
+CHUNK = 512
+N_CHUNKS = N_TOK // CHUNK
+TILES = CHUNK // P
+N_TILES = N_TOK // P
+N_UNITS = N_CHUNKS * S
+
+LAG_S2 = 4
+LAG_TX = 6
+LAST = N_UNITS - 1
+FAST_INTERLEAVE = False
+VECTOR_READS = ()
+
+
+def tile_moe_pb_kernel(tc, encodings, alphas, W1, b1, W2, b2, out):
+    nc = tc.nc
+    with ExitStack() as ctx:
+        const = ctx.enter_context(tc.tile_pool(name="const", bufs=1))
+        xraw_pool = ctx.enter_context(tc.tile_pool(name="xraw", bufs=N_CHUNKS))
+        xtile_pool = ctx.enter_context(tc.tile_pool(name="xtile", bufs=5))
+        xq_pool = ctx.enter_context(tc.tile_pool(name="xq", bufs=3))
+        wraw_pool = ctx.enter_context(tc.tile_pool(name="wraw", bufs=S))
+        wgrp_pool = ctx.enter_context(tc.tile_pool(name="wgrp", bufs=4))
+        rows_pool = ctx.enter_context(tc.tile_pool(name="rows", bufs=4))
+        hgrp_pool = ctx.enter_context(tc.tile_pool(name="hgrp", bufs=3))
+        hq_pool = ctx.enter_context(tc.tile_pool(name="hq", bufs=LAG_S2 + 2))
+        prob_pool = ctx.enter_context(tc.tile_pool(name="prob", bufs=4))
+        mix_pool = ctx.enter_context(tc.tile_pool(name="mix", bufs=3))
+        psum = ctx.enter_context(tc.psum_pool(name="psum", bufs=8))
+        ctx.enter_context(tc.manual_schedule())
+
+        x_raw = []
+        for c in range(N_CHUNKS):
+            x_chunk = xraw_pool.tile([P, TILES, H], BF16, name="x_chunk")
+            x_raw.append(x_chunk)
+        w1_raw = []
+        for s in range(S):
+            w1_rows = wraw_pool.tile([P, PACK, H], BF16, name="w1_rows")
+            w1_raw.append(w1_rows)
+        w2_raw = const.tile([P, S, PACK, T], BF16, name="w2_raw")
+        b1_raw = const.tile([P, S, PACK], BF16, name="b1_raw")
+        b2_raw = const.tile([P, S], BF16, name="b2_raw")
+        al_raw = const.tile([P, P], BF16, name="al_raw")
+
+        def load_x(c, pieces):
+            rows = encodings[c * CHUNK : (c + 1) * CHUNK, :].rearrange("(j p) f -> p j f", p=P)
+            step = TILES // pieces
+            for i in range(pieces):
+                nc.sync.dma_start(
+                    out=x_raw[c][:, i * step : (i + 1) * step, :], in_=rows[:, i * step : (i + 1) * step, :]
+                )
+
+        def load_w1(s):
+            nc.sync.dma_start(out=w1_raw[s][:], in_=W1[s].rearrange("(p j) c -> p j c", j=PACK))
+
+        load_x(0, TILES)
+        nc.sync.dma_start(out=al_raw[:], in_=alphas.rearrange("s (g i) -> (s g) i", i=P))
+        load_w1(0)
+        nc.sync.dma_start(out=b1_raw[:], in_=b1.rearrange("s (p t) -> p s t", t=PACK))
+        load_x(1, 1)
+        load_w1(1)
+        load_w1(2)
+        load_x(2, 1)
+        load_w1(3)
+        nc.sync.dma_start(
+            out=w2_raw[:].rearrange("p s j c -> p s (j c)"), in_=W2.rearrange("s (p j) c -> p s (j c)", j=PACK)
+        )
+        with nc.allow_non_contiguous_dma(reason="b2 is 512 values, one to a partition for each source"):
+            nc.sync.dma_start(out=b2_raw[:], in_=b2.rearrange("s c -> c s"))
+        for c in range(3, N_CHUNKS):
+            load_x(c, 1)
+
+        ident = const.tile([P, P], F32, name="ident")
+        masks.make_identity(nc, ident[:])
+        warm_in = const.tile([P, 1], F32, name="warm_in")
+        warm_out = const.tile([P, 1], F32, name="warm_out")
+        nc.vector.memset(warm_in[:], 0.0)
+        nc.scalar.activation(out=warm_out[:], in_=warm_in[:], func=ACT.Sigmoid)
+
+        b1_col = const.tile([P, S * PACK], F32, name="b1_col")
+        b2_col = const.tile([P, S], F32, name="b2_col")
+        al_f32 = const.tile([P, P], F32, name="al_f32")
+        al_col = const.tile([P, P], F32, name="al_col")
+
+        w1_codes = []
+        w1_scales = []
+        for s in range(S):
+            w1c = const.tile([P, H], U32, name="w1c%d" % s, align_bytes=64)
+            w1s = const.tile([P, H], U8, name="w1s%d" % s, align_bytes=64)
+            w1_codes.append(w1c)
+            w1_scales.append(w1s)
+        w2_codes = const.tile([P, S * T], U32, name="w2_codes", align_bytes=64)
+        w2_scales = const.tile([P, S * T], U8, name="w2_scales", align_bytes=64)
+
+        w_grouped = {}
+
+        def w1_copy(s, t):
+            w_grp = wgrp_pool.tile([P, P * PACK], BF16, name="w_grp", align_bytes=64)
+            nc.vector.tensor_copy(
+                out=w_grp[:].rearrange("p (m j) -> p m j", j=PACK),
+                in_=w1_raw[s][:, :, t:H:PACK].rearrange("p j m -> p m j"),
+            )
+            w_grouped[("w1", s, t)] = w_grp
+
+        def w1_quant(s, t):
+            cols = slice(t * P, (t + 1) * P)
+            nc.vector.quantize_mx(
+                out=w1_codes[s][:, cols].bitcast(FP8X4), scales=w1_scales[s][:, cols], in_=w_grouped[("w1", s, t)][:]
+            )
+
+        def w2_copy(s):
+            w_grp = wgrp_pool.tile([P, P * PACK], BF16, name="w_grp", align_bytes=64)
+            nc.vector.tensor_copy(
+                out=w_grp[:].rearrange("p (c j) -> p c j", j=PACK), in_=w2_raw[:, s, :, :].rearrange("p j c -> p c j")
+            )
+            w_grouped[("w2", s)] = w_grp
+
+        def w2_quant(s):
+            cols = slice(s * T, (s + 1) * T)
+            nc.vector.quantize_mx(
+                out=w2_codes[:, cols].bitcast(FP8X4), scales=w2_scales[:, cols], in_=w_grouped[("w2", s)][:]
+            )
+
+        x_relu = {}
+        x_bank = {}
+        x_grp = {}
+        x_codes = {}
+        x_scales = {}
+
+        def relu_x(g):
+            c, j = divmod(g, TILES)
+            x_pos = xtile_pool.tile([P, H], BF16, name="x_pos")
+            nc.vector.tensor_scalar_max(out=x_pos[:], in0=x_raw[c][:, j, :], scalar1=0.0)
+            x_relu[g] = x_pos
+
+        def transpose_x(g):
+            xt = psum.tile([P, 2, P], F32, name="xt", tag="bank")
+            words = x_relu[g][:].bitcast(F32)
+            for u in range(2):
+                nc.tensor.transpose(xt[:, u, :], words[:, u : H // 2 : 2], ident[:])
+            x_bank[g] = xt
+
+        def copy_x(g):
+            x_k4 = xtile_pool.tile([P, P * PACK], BF16, name="x_k4", align_bytes=64)
+            nc.scalar.copy(
+                out=x_k4[:].bitcast(F32).rearrange("p (r u) -> p r u", u=2), in_=x_bank[g][:].rearrange("p u r -> p r u")
+            )
+            x_grp[g] = x_k4
+
+        def quant_x(g):
+            c, j = divmod(g, TILES)
+            if j == 0:
+                xc = xq_pool.tile([P, CHUNK], U32, name="xc", align_bytes=64)
+                xs = xq_pool.tile([P, CHUNK], U8, name="xs", align_bytes=64)
+                x_codes[c] = xc
+                x_scales[c] = xs
+            cols = slice(j * P, (j + 1) * P)
+            nc.vector.quantize_mx(
+                out=x_codes[c][:, cols].bitcast(FP8X4), scales=x_scales[c][:, cols], in_=x_grp[g][:]
+            )
+
+        s1_banks = {}
+        h_rows = {}
+        h_grp = {}
+        h_codes = {}
+        h_scales = {}
+        s2_bank = {}
+        probs = {}
+        mix_bank = {}
+        mixed = {}
+
+        def stage1(k):
+            c, s = divmod(k, S)
+            banks = []
+            for t in range(PACK):
+                cols = slice(t * P, (t + 1) * P)
+                bank = psum.tile([P, CHUNK], F32, name="s1_bank", tag="bank")
+                nc.tensor.matmul_mx(
+                    out=bank[:],
+                    lhsT=w1_codes[s][:, cols].bitcast(FP8X4),
+                    lhsT_scale=w1_scales[s][:, cols],
+                    rhs=x_codes[c][:].bitcast(FP8X4),
+                    rhs_scale=x_scales[c][:],
+                    start=True,
+                    stop=True,
+                )
+                banks.append(bank)
+            s1_banks[k] = banks
+
+        def parts_of(k):
+            return 2 if k == LAST else 1
+
+        def new_rows(k):
+            rows = rows_pool.tile([P, PACK, CHUNK], BF16, name="rows")
+            h_rows[k] = rows
+
+        def bias_relu(k, engine):
+            s = k % S
+            for t in range(PACK):
+                col = s * PACK + t
+                if engine == "scalar" and (s, t) not in VECTOR_READS:
+                    nc.scalar.activation(
+                        out=h_rows[k][:, t, :],
+                        in_=s1_banks[k][t][:],
+                        func=ACT.Relu,
+                        bias=b1_col[:, col : col + 1],
+                        scale=1.0,
+                    )
+                if engine == "vector" and (s, t) in VECTOR_READS:
+                    nc.vector.tensor_scalar(
+                        out=h_rows[k][:, t, :],
+                        in0=s1_banks[k][t][:],
+                        scalar1=b1_col[:, col : col + 1],
+                        scalar2=0.0,
+                        op0=ALU.add,
+                        op1=ALU.max,
+                    )
+
+        def interleave(k):
+            h_k4 = hgrp_pool.tile([P, CHUNK * PACK], BF16, name="h_k4", align_bytes=64)
+            h_grp[k] = h_k4
+            width = CHUNK // parts_of(k)
+            for h in range(parts_of(k)):
+                dst = h_k4[:, h * width * PACK : (h + 1) * width * PACK]
+                src = h_rows[k][:, :, h * width : (h + 1) * width]
+                if FAST_INTERLEAVE:
+                    nc.vector.tensor_copy(
+                        out=dst.rearrange("p (c i t) -> p c t i", i=4, t=PACK),
+                        in_=src.rearrange("p t (c i) -> p c t i", i=4),
+                    )
+                else:
+                    nc.vector.tensor_copy(
+                        out=dst.rearrange("p (n t) -> p n t", t=PACK), in_=src.rearrange("p t n -> p n t")
+                    )
+
+        def quant_h(k):
+            hc = hq_pool.tile([P, CHUNK], U32, name="hc", align_bytes=64)
+            hs = hq_pool.tile([P, CHUNK], U8, name="hs", align_bytes=64)
+            h_codes[k] = hc
+            h_scales[k] = hs
+            width = CHUNK // parts_of(k)
+            for h in range(parts_of(k)):
+                cols = slice(h * width, (h + 1) * width)
+                nc.vector.quantize_mx(
+                    out=hc[:, cols].bitcast(FP8X4),
+                    scales=hs[:, cols],
+                    in_=h_grp[k][:, h * width * PACK : (h + 1) * width * PACK],
+                )
+
+        def stage2(k):
+            s = k % S
+            w_cols = slice(s * T, (s + 1) * T)
+            width = CHUNK // parts_of(k)
+            s2_bank[k] = []
+            for h in range(parts_of(k)):
+                cols = slice(h * width, (h + 1) * width)
+                bank = psum.tile([P, width], F32, name="s2_bank", tag="bank")
+                nc.tensor.matmul_mx(
+                    out=bank[:],
+                    lhsT=w2_codes[:, w_cols].bitcast(FP8X4),
+                    lhsT_scale=w2_scales[:, w_cols],
+                    rhs=h_codes[k][:, cols].bitcast(FP8X4),
+                    rhs_scale=h_scales[k][:, cols],
+                    start=True,
+                    stop=True,
+                )
+                s2_bank[k].append(bank)
+
+        def sigmoid(k):
+            s = k % S
+            prob = prob_pool.tile([P, CHUNK], F32, name="prob")
+            probs[k] = prob
+            width = CHUNK // parts_of(k)
+            for h in range(parts_of(k)):
+                nc.scalar.activation(
+                    out=prob[:, h * width : (h + 1) * width],
+                    in_=s2_bank[k][h][:],
+                    func=ACT.Sigmoid,
+                    bias=b2_col[:, s : s + 1],
+                    scale=1.0,
+                )
+
+        def transpose_p(k):
+            per = TILES // parts_of(k)
+            mix_bank[k] = []
+            for h in range(parts_of(k)):
+                pt = psum.tile([P, per, T], F32, name="pt", tag="bank")
+                for i in range(per):
+                    j = h * per + i
+                    nc.tensor.transpose(pt[:, i, :], probs[k][:, j * P : (j + 1) * P], ident[:])
+                mix_bank[k].append(pt)
+
+        def mix(k):
+            c, s = divmod(k, S)
+            per = TILES // parts_of(k)
+            if s == 0:
+                acc = mix_pool.tile([P, TILES, T], F32, name="acc")
+                mixed[c] = acc
+            rows_out = out[c * CHUNK : (c + 1) * CHUNK, :].rearrange("(j p) t -> p j t", p=P)
+            for j in range(TILES):
+                col = s * N_TILES + c * TILES + j
+                turned = mix_bank[k][j // per][:, j % per, :]
+                if s == 0:
+                    nc.vector.tensor_scalar_mul(out=mixed[c][:, j, :], in0=turned, scalar1=al_col[:, col : col + 1])
+                else:
+                    nc.vector.scalar_tensor_tensor(
+                        out=mixed[c][:, j, :],
+                        in0=turned,
+                        scalar=al_col[:, col : col + 1],
+                        in1=mixed[c][:, j, :],
+                        op0=ALU.mult,
+                        op1=ALU.add,
+                    )
+                if k == LAST:
+                    nc.sync.dma_start(out=rows_out[:, j, :], in_=mixed[c][:, j, :])
+            if s == S - 1 and k != LAST:
+                nc.sync.dma_start(out=rows_out, in_=mixed[c][:])
+
+        for g in range(TILES):
+            relu_x(g)
+            transpose_x(g)
+            copy_x(g)
+        nc.scalar.copy(out=al_f32[:], in_=al_raw[:])
+        al_bank = psum.tile([P, P], F32, name="al_bank", tag="bank")
+        nc.tensor.transpose(al_bank[:], al_f32[:], ident[:])
+        nc.scalar.copy(out=al_col[:], in_=al_bank[:])
+        for g in range(TILES):
+            quant_x(g)
+
+        def prepare(jobs):
+            waiting = None
+            for kind, s, t in jobs:
+                if kind == "w1":
+                    w1_copy(s, t)
+                else:
+                    w2_copy(s)
+                if waiting is not None:
+                    prepare_quant(waiting)
+                waiting = (kind, s, t)
+            if waiting is not None:
+                prepare_quant(waiting)
+
+        def prepare_quant(job):
+            kind, s, t = job
+            if kind == "w1":
+                w1_quant(s, t)
+            else:
+                w2_quant(s)
+
+        w1_copy(0, 0)
+        nc.vector.tensor_copy(out=b1_col[:], in_=b1_raw[:].rearrange("p s t -> p (s t)"))
+        w1_copy(0, 1)
+        w1_quant(0, 0)
+        w1_copy(0, 2)
+        w1_quant(0, 1)
+        w1_copy(0, 3)
+        w1_quant(0, 2)
+        for g in range(TILES, LAG_TX + 2):
+            relu_x(g)
+        w1_quant(0, 3)
+
+        prep = [("w1", s, t) for s in range(1, S) for t in range(PACK)] + [("w2", s, 0) for s in range(S)]
+        prep_per_step = [12, 0, 2, 2]
+
+        s2_at = {}
+        for u in range(N_UNITS):
+            step = min(u + LAG_S2, N_UNITS) if u < LAST else N_UNITS + 1
+            s2_at.setdefault(step, []).append(u)
+
+        for k in range(N_UNITS + 3):
+            if k < N_UNITS:
+                stage1(k)
+                new_rows(k)
+                bias_relu(k, "scalar")
+            for u in s2_at.get(k, []):
+                stage2(u)
+                sigmoid(u)
+            new_tiles = list(range(TILES, LAG_TX + 1)) if k == 0 else [k + LAG_TX]
+            new_tiles = [g for g in new_tiles if g < N_TILES]
+            for g in new_tiles:
+                transpose_x(g)
+                copy_x(g)
+            for u in s2_at.get(k - 1, []):
+                transpose_p(u)
+
+            old_tiles = list(range(TILES, LAG_TX + 1)) if k == 1 else ([k + LAG_TX - 1] if k > 1 else [])
+            for g in old_tiles:
+                if g < N_TILES:
+                    quant_x(g)
+            if 0 <= k - 1 < N_UNITS:
+                interleave(k - 1)
+            if k - 1 == LAST:
+                quant_h(k - 1)
+            if k < N_UNITS:
+                bias_relu(k, "vector")
+            jobs = prep[: prep_per_step[k]] if k < len(prep_per_step) else []
+            prep = prep[len(jobs) :]
+            prepare(jobs)
+            if k == 2:
+                nc.vector.tensor_copy(out=b2_col[:], in_=b2_raw[:])
+            for u in s2_at.get(k - 1, []):
+                mix(u)
+            if k + LAG_TX + 2 < N_TILES:
+                relu_x(k + LAG_TX + 2)
+            if 0 <= k - 1 < LAST:
+                quant_h(k - 1)

@@ -25,8 +25,8 @@ N_UNITS = N_CHUNKS * S
 LAG_S2 = 4
 LAG_TX = 6
 LAST = N_UNITS - 1
-FAST_INTERLEAVE = False
-VECTOR_READS = ()
+FAST_INTERLEAVE = True
+VECTOR_READS = ((3, 3),)
 
 
 def tile_moe_pb_kernel(tc, encodings, alphas, W1, b1, W2, b2, out):

from contextlib import ExitStack

import concourse.masks as masks
import concourse.mybir as mybir

N_TOK, H, S, T = 4096, 512, 4, 128
FLOPS = 2 * N_TOK * H * H * S + 2 * N_TOK * H * T * S

F32 = mybir.dt.float32
BF16 = mybir.dt.bfloat16
U32 = mybir.dt.uint32
U8 = mybir.dt.uint8
FP8X4 = mybir.dt.float8_e4m3fn_x4
ACT = mybir.ActivationFunctionType
ALU = mybir.AluOpType

P = 128
PACK = 4
CHUNK = 512
N_CHUNKS = N_TOK // CHUNK
TILES = CHUNK // P
N_TILES = N_TOK // P
N_UNITS = N_CHUNKS * S

LAG_S2 = 4
LAG_TX = 6
LAST = N_UNITS - 1
FAST_INTERLEAVE = True
VECTOR_READS = ((3, 3),)


def tile_moe_pb_kernel(tc, encodings, alphas, W1, b1, W2, b2, out):
    nc = tc.nc
    with ExitStack() as ctx:
        const = ctx.enter_context(tc.tile_pool(name="const", bufs=1))
        xraw_pool = ctx.enter_context(tc.tile_pool(name="xraw", bufs=N_CHUNKS))
        xtile_pool = ctx.enter_context(tc.tile_pool(name="xtile", bufs=5))
        xq_pool = ctx.enter_context(tc.tile_pool(name="xq", bufs=3))
        wraw_pool = ctx.enter_context(tc.tile_pool(name="wraw", bufs=S))
        wgrp_pool = ctx.enter_context(tc.tile_pool(name="wgrp", bufs=4))
        rows_pool = ctx.enter_context(tc.tile_pool(name="rows", bufs=4))
        hgrp_pool = ctx.enter_context(tc.tile_pool(name="hgrp", bufs=3))
        hq_pool = ctx.enter_context(tc.tile_pool(name="hq", bufs=LAG_S2 + 2))
        prob_pool = ctx.enter_context(tc.tile_pool(name="prob", bufs=4))
        mix_pool = ctx.enter_context(tc.tile_pool(name="mix", bufs=3))
        psum = ctx.enter_context(tc.psum_pool(name="psum", bufs=8))
        ctx.enter_context(tc.manual_schedule())

        x_raw = []
        for c in range(N_CHUNKS):
            x_chunk = xraw_pool.tile([P, TILES, H], BF16, name="x_chunk")
            x_raw.append(x_chunk)
        w1_raw = []
        for s in range(S):
            w1_rows = wraw_pool.tile([P, PACK, H], BF16, name="w1_rows")
            w1_raw.append(w1_rows)
        w2_raw = const.tile([P, S, PACK, T], BF16, name="w2_raw")
        b1_raw = const.tile([P, S, PACK], BF16, name="b1_raw")
        b2_raw = const.tile([P, S], BF16, name="b2_raw")
        al_raw = const.tile([P, P], BF16, name="al_raw")

        def load_x(c, pieces):
            rows = encodings[c * CHUNK : (c + 1) * CHUNK, :].rearrange("(j p) f -> p j f", p=P)
            step = TILES // pieces
            for i in range(pieces):
                nc.sync.dma_start(
                    out=x_raw[c][:, i * step : (i + 1) * step, :], in_=rows[:, i * step : (i + 1) * step, :]
                )

        def load_w1(s):
            nc.sync.dma_start(out=w1_raw[s][:], in_=W1[s].rearrange("(p j) c -> p j c", j=PACK))

        load_x(0, TILES)
        nc.sync.dma_start(out=al_raw[:], in_=alphas.rearrange("s (g i) -> (s g) i", i=P))
        load_w1(0)
        nc.sync.dma_start(out=b1_raw[:], in_=b1.rearrange("s (p t) -> p s t", t=PACK))
        load_x(1, 1)
        load_w1(1)
        load_w1(2)
        load_x(2, 1)
        load_w1(3)
        nc.sync.dma_start(
            out=w2_raw[:].rearrange("p s j c -> p s (j c)"), in_=W2.rearrange("s (p j) c -> p s (j c)", j=PACK)
        )
        with nc.allow_non_contiguous_dma(reason="b2 is 512 values, one to a partition for each source"):
            nc.sync.dma_start(out=b2_raw[:], in_=b2.rearrange("s c -> c s"))
        for c in range(3, N_CHUNKS):
            load_x(c, 1)

        ident = const.tile([P, P], F32, name="ident")
        masks.make_identity(nc, ident[:])
        warm_in = const.tile([P, 1], F32, name="warm_in")
        warm_out = const.tile([P, 1], F32, name="warm_out")
        nc.vector.memset(warm_in[:], 0.0)
        nc.scalar.activation(out=warm_out[:], in_=warm_in[:], func=ACT.Sigmoid)

        b1_col = const.tile([P, S * PACK], F32, name="b1_col")
        b2_col = const.tile([P, S], F32, name="b2_col")
        al_f32 = const.tile([P, P], F32, name="al_f32")
        al_col = const.tile([P, P], F32, name="al_col")

        w1_codes = []
        w1_scales = []
        for s in range(S):
            w1c = const.tile([P, H], U32, name="w1c%d" % s, align_bytes=64)
            w1s = const.tile([P, H], U8, name="w1s%d" % s, align_bytes=64)
            w1_codes.append(w1c)
            w1_scales.append(w1s)
        w2_codes = const.tile([P, S * T], U32, name="w2_codes", align_bytes=64)
        w2_scales = const.tile([P, S * T], U8, name="w2_scales", align_bytes=64)

        w_grouped = {}

        def w1_copy(s, t):
            w_grp = wgrp_pool.tile([P, P * PACK], BF16, name="w_grp", align_bytes=64)
            nc.vector.tensor_copy(
                out=w_grp[:].rearrange("p (m j) -> p m j", j=PACK),
                in_=w1_raw[s][:, :, t:H:PACK].rearrange("p j m -> p m j"),
            )
            w_grouped[("w1", s, t)] = w_grp

        def w1_quant(s, t):
            cols = slice(t * P, (t + 1) * P)
            nc.vector.quantize_mx(
                out=w1_codes[s][:, cols].bitcast(FP8X4), scales=w1_scales[s][:, cols], in_=w_grouped[("w1", s, t)][:]
            )

        def w2_copy(s):
            w_grp = wgrp_pool.tile([P, P * PACK], BF16, name="w_grp", align_bytes=64)
            nc.vector.tensor_copy(
                out=w_grp[:].rearrange("p (c j) -> p c j", j=PACK), in_=w2_raw[:, s, :, :].rearrange("p j c -> p c j")
            )
            w_grouped[("w2", s)] = w_grp

        def w2_quant(s):
            cols = slice(s * T, (s + 1) * T)
            nc.vector.quantize_mx(
                out=w2_codes[:, cols].bitcast(FP8X4), scales=w2_scales[:, cols], in_=w_grouped[("w2", s)][:]
            )

        x_relu = {}
        x_bank = {}
        x_grp = {}
        x_codes = {}
        x_scales = {}

        def relu_x(g):
            c, j = divmod(g, TILES)
            x_pos = xtile_pool.tile([P, H], BF16, name="x_pos")
            nc.vector.tensor_scalar_max(out=x_pos[:], in0=x_raw[c][:, j, :], scalar1=0.0)
            x_relu[g] = x_pos

        def transpose_x(g):
            xt = psum.tile([P, 2, P], F32, name="xt", tag="bank")
            words = x_relu[g][:].bitcast(F32)
            for u in range(2):
                nc.tensor.transpose(xt[:, u, :], words[:, u : H // 2 : 2], ident[:])
            x_bank[g] = xt

        def copy_x(g):
            x_k4 = xtile_pool.tile([P, P * PACK], BF16, name="x_k4", align_bytes=64)
            nc.scalar.copy(
                out=x_k4[:].bitcast(F32).rearrange("p (r u) -> p r u", u=2), in_=x_bank[g][:].rearrange("p u r -> p r u")
            )
            x_grp[g] = x_k4

        def quant_x(g):
            c, j = divmod(g, TILES)
            if j == 0:
                xc = xq_pool.tile([P, CHUNK], U32, name="xc", align_bytes=64)
                xs = xq_pool.tile([P, CHUNK], U8, name="xs", align_bytes=64)
                x_codes[c] = xc
                x_scales[c] = xs
            cols = slice(j * P, (j + 1) * P)
            nc.vector.quantize_mx(
                out=x_codes[c][:, cols].bitcast(FP8X4), scales=x_scales[c][:, cols], in_=x_grp[g][:]
            )

        s1_banks = {}
        h_rows = {}
        h_grp = {}
        h_codes = {}
        h_scales = {}
        s2_bank = {}
        probs = {}
        mix_bank = {}
        mixed = {}

        def stage1(k):
            c, s = divmod(k, S)
            banks = []
            for t in range(PACK):
                cols = slice(t * P, (t + 1) * P)
                bank = psum.tile([P, CHUNK], F32, name="s1_bank", tag="bank")
                nc.tensor.matmul_mx(
                    out=bank[:],
                    lhsT=w1_codes[s][:, cols].bitcast(FP8X4),
                    lhsT_scale=w1_scales[s][:, cols],
                    rhs=x_codes[c][:].bitcast(FP8X4),
                    rhs_scale=x_scales[c][:],
                    start=True,
                    stop=True,
                )
                banks.append(bank)
            s1_banks[k] = banks

        def parts_of(k):
            return 2 if k == LAST else 1

        def new_rows(k):
            rows = rows_pool.tile([P, PACK, CHUNK], BF16, name="rows")
            h_rows[k] = rows

        def bias_relu(k, engine):
            s = k % S
            for t in range(PACK):
                col = s * PACK + t
                if engine == "scalar" and (s, t) not in VECTOR_READS:
                    nc.scalar.activation(
                        out=h_rows[k][:, t, :],
                        in_=s1_banks[k][t][:],
                        func=ACT.Relu,
                        bias=b1_col[:, col : col + 1],
                        scale=1.0,
                    )
                if engine == "vector" and (s, t) in VECTOR_READS:
                    nc.vector.tensor_scalar(
                        out=h_rows[k][:, t, :],
                        in0=s1_banks[k][t][:],
                        scalar1=b1_col[:, col : col + 1],
                        scalar2=0.0,
                        op0=ALU.add,
                        op1=ALU.max,
                    )

        def interleave(k):
            h_k4 = hgrp_pool.tile([P, CHUNK * PACK], BF16, name="h_k4", align_bytes=64)
            h_grp[k] = h_k4
            width = CHUNK // parts_of(k)
            for h in range(parts_of(k)):
                dst = h_k4[:, h * width * PACK : (h + 1) * width * PACK]
                src = h_rows[k][:, :, h * width : (h + 1) * width]
                if FAST_INTERLEAVE:
                    nc.vector.tensor_copy(
                        out=dst.rearrange("p (c i t) -> p c t i", i=4, t=PACK),
                        in_=src.rearrange("p t (c i) -> p c t i", i=4),
                    )
                else:
                    nc.vector.tensor_copy(
                        out=dst.rearrange("p (n t) -> p n t", t=PACK), in_=src.rearrange("p t n -> p n t")
                    )

        def quant_h(k):
            hc = hq_pool.tile([P, CHUNK], U32, name="hc", align_bytes=64)
            hs = hq_pool.tile([P, CHUNK], U8, name="hs", align_bytes=64)
            h_codes[k] = hc
            h_scales[k] = hs
            width = CHUNK // parts_of(k)
            for h in range(parts_of(k)):
                cols = slice(h * width, (h + 1) * width)
                nc.vector.quantize_mx(
                    out=hc[:, cols].bitcast(FP8X4),
                    scales=hs[:, cols],
                    in_=h_grp[k][:, h * width * PACK : (h + 1) * width * PACK],
                )

        def stage2(k):
            s = k % S
            w_cols = slice(s * T, (s + 1) * T)
            width = CHUNK // parts_of(k)
            s2_bank[k] = []
            for h in range(parts_of(k)):
                cols = slice(h * width, (h + 1) * width)
                bank = psum.tile([P, width], F32, name="s2_bank", tag="bank")
                nc.tensor.matmul_mx(
                    out=bank[:],
                    lhsT=w2_codes[:, w_cols].bitcast(FP8X4),
                    lhsT_scale=w2_scales[:, w_cols],
                    rhs=h_codes[k][:, cols].bitcast(FP8X4),
                    rhs_scale=h_scales[k][:, cols],
                    start=True,
                    stop=True,
                )
                s2_bank[k].append(bank)

        def sigmoid(k):
            s = k % S
            prob = prob_pool.tile([P, CHUNK], F32, name="prob")
            probs[k] = prob
            width = CHUNK // parts_of(k)
            for h in range(parts_of(k)):
                nc.scalar.activation(
                    out=prob[:, h * width : (h + 1) * width],
                    in_=s2_bank[k][h][:],
                    func=ACT.Sigmoid,
                    bias=b2_col[:, s : s + 1],
                    scale=1.0,
                )

        def transpose_p(k):
            per = TILES // parts_of(k)
            mix_bank[k] = []
            for h in range(parts_of(k)):
                pt = psum.tile([P, per, T], F32, name="pt", tag="bank")
                for i in range(per):
                    j = h * per + i
                    nc.tensor.transpose(pt[:, i, :], probs[k][:, j * P : (j + 1) * P], ident[:])
                mix_bank[k].append(pt)

        def mix(k):
            c, s = divmod(k, S)
            per = TILES // parts_of(k)
            if s == 0:
                acc = mix_pool.tile([P, TILES, T], F32, name="acc")
                mixed[c] = acc
            rows_out = out[c * CHUNK : (c + 1) * CHUNK, :].rearrange("(j p) t -> p j t", p=P)
            for j in range(TILES):
                col = s * N_TILES + c * TILES + j
                turned = mix_bank[k][j // per][:, j % per, :]
                if s == 0:
                    nc.vector.tensor_scalar_mul(out=mixed[c][:, j, :], in0=turned, scalar1=al_col[:, col : col + 1])
                else:
                    nc.vector.scalar_tensor_tensor(
                        out=mixed[c][:, j, :],
                        in0=turned,
                        scalar=al_col[:, col : col + 1],
                        in1=mixed[c][:, j, :],
                        op0=ALU.mult,
                        op1=ALU.add,
                    )
                if k == LAST:
                    nc.sync.dma_start(out=rows_out[:, j, :], in_=mixed[c][:, j, :])
            if s == S - 1 and k != LAST:
                nc.sync.dma_start(out=rows_out, in_=mixed[c][:])

        for g in range(TILES):
            relu_x(g)
            transpose_x(g)
            copy_x(g)
        nc.scalar.copy(out=al_f32[:], in_=al_raw[:])
        al_bank = psum.tile([P, P], F32, name="al_bank", tag="bank")
        nc.tensor.transpose(al_bank[:], al_f32[:], ident[:])
        nc.scalar.copy(out=al_col[:], in_=al_bank[:])
        for g in range(TILES):
            quant_x(g)

        def prepare(jobs):
            waiting = None
            for kind, s, t in jobs:
                if kind == "w1":
                    w1_copy(s, t)
                else:
                    w2_copy(s)
                if waiting is not None:
                    prepare_quant(waiting)
                waiting = (kind, s, t)
            if waiting is not None:
                prepare_quant(waiting)

        def prepare_quant(job):
            kind, s, t = job
            if kind == "w1":
                w1_quant(s, t)
            else:
                w2_quant(s)

        w1_copy(0, 0)
        nc.vector.tensor_copy(out=b1_col[:], in_=b1_raw[:].rearrange("p s t -> p (s t)"))
        w1_copy(0, 1)
        w1_quant(0, 0)
        w1_copy(0, 2)
        w1_quant(0, 1)
        w1_copy(0, 3)
        w1_quant(0, 2)
        for g in range(TILES, LAG_TX + 2):
            relu_x(g)
        w1_quant(0, 3)

        prep = [("w1", s, t) for s in range(1, S) for t in range(PACK)] + [("w2", s, 0) for s in range(S)]
        prep_per_step = [12, 0, 2, 2]

        s2_at = {}
        for u in range(N_UNITS):
            step = min(u + LAG_S2, N_UNITS) if u < LAST else N_UNITS + 1
            s2_at.setdefault(step, []).append(u)

        for k in range(N_UNITS + 3):
            if k < N_UNITS:
                stage1(k)
                new_rows(k)
                bias_relu(k, "scalar")
            for u in s2_at.get(k, []):
                stage2(u)
                sigmoid(u)
            new_tiles = list(range(TILES, LAG_TX + 1)) if k == 0 else [k + LAG_TX]
            new_tiles = [g for g in new_tiles if g < N_TILES]
            for g in new_tiles:
                transpose_x(g)
                copy_x(g)
            for u in s2_at.get(k - 1, []):
                transpose_p(u)

            old_tiles = list(range(TILES, LAG_TX + 1)) if k == 1 else ([k + LAG_TX - 1] if k > 1 else [])
            for g in old_tiles:
                if g < N_TILES:
                    quant_x(g)
            if 0 <= k - 1 < N_UNITS:
                interleave(k - 1)
            if k - 1 == LAST:
                quant_h(k - 1)
            if k < N_UNITS:
                bias_relu(k, "vector")
            jobs = prep[: prep_per_step[k]] if k < len(prep_per_step) else []
            prep = prep[len(jobs) :]
            prepare(jobs)
            if k == 2:
                nc.vector.tensor_copy(out=b2_col[:], in_=b2_raw[:])
            for u in s2_at.get(k - 1, []):
                mix(u)
            if k + LAG_TX + 2 < N_TILES:
                relu_x(k + LAG_TX + 2)
            if 0 <= k - 1 < LAST:
                quant_h(k - 1)
